import numpy as np
import ml_dtypes


def mxq(x, axis, fmt="e4m3"):
    dtype, down = {"e4m3": (ml_dtypes.float8_e4m3fn, 7), "e5m2": (ml_dtypes.float8_e5m2, 14)}[fmt]
    v = np.moveaxis(np.asarray(x, np.float32).astype(ml_dtypes.bfloat16).astype(np.float64), axis, -1)
    blocks = v.reshape(v.shape[:-1] + (-1, 32))
    amax = np.abs(blocks).max(-1, keepdims=True)
    byte = np.maximum(np.where(amax > 0, np.frexp(amax)[1] - 1 + 127, 0) - down, 1)
    scale = np.exp2(byte - 127.0)
    codes = (blocks / scale).astype(np.float32).astype(dtype).astype(np.float64)
    return np.moveaxis((codes * scale).reshape(v.shape), -1, axis)


WIDE = False


def mx_kscale(k):
    if not WIDE:
        return np.ones(k)
    levels = np.array([10, -10, 5, -5, 0])
    if k % 512:
        return np.exp2(np.random.permutation(np.resize(levels, k // 32))).repeat(32)
    a = np.empty((k // 512, 16))
    for p in range(k // 512):
        a[p, :8] = np.random.permutation(np.resize(levels, 8))
        for g in range(8):
            far = levels[np.abs(levels - a[p, g]) >= 10]
            a[p, g + 8] = far[np.random.randint(len(far))]
    return np.exp2(a.ravel()).repeat(32)


BF16 = ml_dtypes.bfloat16


def bf(x):
    return np.asarray(x, np.float32).astype(BF16)


def f64(x):
    return np.asarray(x).astype(np.float64)


B, C, H, W, DM, GH = 6, 512, 32, 32, 128, 512


def sigmoid(v):
    return 1.0 / (1.0 + np.exp(-v))


def draw0():
    s = np.concatenate([mx_kscale(C), np.ones(C)])
    t = mx_kscale(GH)
    return {'x': bf(np.random.standard_normal((B, C, H, W)) * s[:C][None, :, None, None]),
            'agg': bf(np.random.standard_normal((B, C, H, W)) * 0.7),
            'g1w': bf(np.random.standard_normal((GH, 2 * C)) / np.sqrt(2 * C) * t[:, None] / s[None, :]),
            'g1b': bf(np.random.standard_normal(GH) * 0.3 * t),
            'g2w': bf(np.random.standard_normal((C, GH)) * 2.0 / np.sqrt(GH) / t[None, :]),
            'g2b': bf(np.random.standard_normal(C) * 0.3)}


def core(x, agg, g1w, g1b, g2w, g2b):
    a = f64(agg).reshape(B, C, H * W)
    cat = np.concatenate([f64(x).reshape(B, C, H * W), a], axis=1)
    hidden = np.maximum((mxq(f64(g1w), 1, 'e4m3') @ mxq(cat, 1, 'e4m3')) + f64(g1b)[None, :, None], 0.0)
    gate = sigmoid((mxq(f64(g2w), 1, 'e4m3') @ mxq(hidden, 1, 'e4m3')) + f64(g2b)[None, :, None])
    return (a * gate).reshape(B, C, H, W)


def e4m3fn_bytes(y):
    return np.clip(np.asarray(y, np.float64), -448.0, 448.0).astype(np.float32).astype(ml_dtypes.float8_e4m3fn).view(np.uint8)


def e4m3fn_values(b):
    return np.asarray(b, np.uint8).view(ml_dtypes.float8_e4m3fn).astype(np.float64)


def setup_inputs():
    d = draw0()
    x0 = np.asarray(d['x']).astype(np.float64)
    s = (np.max(np.abs(x0), axis=(0, 2, 3), keepdims=True) / 448.0).astype(np.float32)
    out = {}
    for k, v in d.items():
        if k == 'x':
            out['x_bytes'] = e4m3fn_bytes(x0 / s.astype(np.float64))
            out['x_scale'] = s
        else:
            out[k] = v
    return out


def reference(x_bytes, x_scale, agg, g1w, g1b, g2w, g2b):
    return core(e4m3fn_values(x_bytes) * x_scale.astype(np.float64), agg, g1w, g1b, g2w, g2b)

@@ -1,0 +1,299 @@
+from contextlib import ExitStack
+
+import concourse.mybir as mybir
+from concourse.masks import make_identity
+
+IMAGES, CH, ROWS, COLS = 6, 512, 32, 32
+PIX = ROWS * COLS
+HID = 512
+FLOPS = 2 * IMAGES * PIX * (HID * 2 * CH + CH * HID)
+
+F32 = mybir.dt.float32
+BF16 = mybir.dt.bfloat16
+U32 = mybir.dt.uint32
+U8 = mybir.dt.uint8
+FP8 = mybir.dt.float8_e4m3fn
+FP8X4 = mybir.dt.float8_e4m3fn_x4
+ACT = mybir.ActivationFunctionType
+ALU = mybir.AluOpType
+
+P = 128
+T4 = 4
+HALF = 512
+HALVES = IMAGES * 2
+S_PLANES = 2
+
+
+def tile_graphaugmentation_pb_t_kernel(tc, x_bytes, x_scale, agg, g1w, g1b, g2w, g2b, out):
+    nc = tc.nc
+    with ExitStack() as ctx:
+        keep = ctx.enter_context(tc.tile_pool(name="keep", bufs=1))
+        sb = ctx.enter_context(tc.tile_pool(name="sb", bufs=2))
+        ps = ctx.enter_context(tc.psum_pool(name="ps", bufs=1))
+        ctx.enter_context(tc.manual_schedule())
+
+        def sbt(tag, shape, dtype, bufs):
+            return sb.tile(shape, dtype, name=tag, tag=tag, bufs=bufs, align_bytes=64)
+
+        def pst(tag, shape, dtype, bufs):
+            return ps.tile(shape, dtype, name=tag, tag=tag, bufs=bufs)
+
+        xb, ag, xs, xi, ai, cx, sx, ca, sa = {}, {}, {}, {}, {}, {}, {}, {}, {}
+        hp, hi, ch, sh, gt, ph, pg, pa = {}, {}, {}, {}, {}, {}, {}, {}
+
+        def load_x(b, pieces=1):
+            xb[b] = sbt("xb", [P, T4, PIX], U8, 3)
+            src = x_bytes[b].rearrange("(p t) h w -> p t (h w)", t=T4)
+            n = T4 // pieces
+            for i in range(pieces):
+                nc.sync.dma_start(out=xb[b][:, i * n:(i + 1) * n, :], in_=src[:, i * n:(i + 1) * n, :])
+
+        def load_agg(b, pieces=1):
+            ag[b] = sbt("ag", [P, T4, PIX], BF16, 4)
+            src = agg[b].rearrange("(p t) h w -> p t (h w)", t=T4)
+            n = PIX // pieces
+            for i in range(pieces):
+                nc.sync.dma_start(out=ag[b][:, :, i * n:(i + 1) * n], in_=src[:, :, i * n:(i + 1) * n])
+
+        xsc = keep.tile([P, T4], F32, name="xsc")
+        b1h = keep.tile([P, T4], BF16, name="b1h")
+        b2h = keep.tile([P, T4], BF16, name="b2h")
+        b1 = keep.tile([P, T4], F32, name="b1")
+        b2 = keep.tile([P, T4], F32, name="b2")
+        w1 = keep.tile([P, T4, 2 * CH], BF16, name="w1", align_bytes=64)
+        w2 = keep.tile([P, T4, HID], BF16, name="w2", align_bytes=64)
+        cw1 = keep.tile([P, 2, HID], U32, name="cw1", align_bytes=64)
+        sw1 = keep.tile([P, 2, HID], U8, name="sw1", align_bytes=64)
+        cw2 = keep.tile([P, CH], U32, name="cw2", align_bytes=64)
+        sw2 = keep.tile([P, CH], U8, name="sw2", align_bytes=64)
+        idf = keep.tile([P, P], F32, name="idf", align_bytes=64)
+        idb = keep.tile([P, P], BF16, name="idb", align_bytes=64)
+        warm = keep.tile([P, 1], F32, name="warm")
+
+        nc.sync.dma_start(out=xsc[:], in_=x_scale.rearrange("o (p t) h w -> p (o t h w)", t=T4))
+        load_x(0, 4)
+        nc.sync.dma_start(out=w1[:], in_=g1w.rearrange("(m t) k -> m t k", t=T4))
+        load_agg(0, 2)
+        nc.sync.dma_start(out=b1h[:], in_=g1b.rearrange("(p t) -> p t", t=T4))
+        nc.sync.dma_start(out=b2h[:], in_=g2b.rearrange("(p t) -> p t", t=T4))
+        load_x(1)
+        nc.sync.dma_start(out=w2[:], in_=g2w.rearrange("(m t) k -> m t k", t=T4))
+        load_agg(1)
+        load_x(2)
+        load_agg(2)
+        load_agg(3)
+
+        nc.gpsimd.memset(warm[:], 0.0)
+        nc.scalar.activation(out=warm[:], in_=warm[:], func=ACT.Sigmoid)
+        make_identity(nc, idf[:])
+        make_identity(nc, idb[:])
+
+        def new_xs(b):
+            xs[b] = sbt("xs", [P, T4, PIX], BF16, 2)
+
+        def widen(eng, b, t, c0, c1):
+            src = xb[b][:, t, c0:c1].bitcast(FP8)
+            dst = xs[b][:, t, c0:c1]
+            if eng == "s":
+                nc.scalar.activation(out=dst, in_=src, func=ACT.Copy, scale=xsc[:, t:t + 1])
+            else:
+                nc.vector.tensor_scalar(out=dst, in0=src, scalar1=xsc[:, t:t + 1], scalar2=None, op0=ALU.mult)
+
+        def interleave(dst, src):
+            nc.vector.tensor_copy(
+                out=dst.rearrange("p (c i t) -> p c t i", i=4, t=T4),
+                in_=src.rearrange("p t (c i) -> p c t i", i=4))
+
+        def x_inter(j):
+            b, c0 = j // 2, (j % 2) * HALF
+            xi[j] = sbt("xi", [P, HALF * T4], BF16, 3)
+            interleave(xi[j][:], xs[b][:, :, c0:c0 + HALF])
+
+        def quant(codes, scales, src):
+            nc.vector.quantize_mx(out=codes.bitcast(FP8X4), scales=scales, in_=src)
+
+        def x_quant(j):
+            cx[j] = sbt("cx", [P, HALF], U32, 4)
+            sx[j] = sbt("sx", [P, HALF], U8, 4)
+            quant(cx[j][:], sx[j][:], xi[j][:])
+
+        def a_fill(j, q, tag="pa", bufs=1):
+            b, c0 = j // 2, (j % 2) * HALF + q * 256
+            bank = pst(tag, [P, 1024], BF16, bufs)
+            pa[(j, q)] = bank
+            for r in range(2):
+                cols = slice(c0 + r * P, c0 + r * P + P)
+                nc.tensor.matmul(
+                    out=bank[:, r * 512:(r + 1) * 512].rearrange("p (n t) -> p n t", t=T4),
+                    lhsT=idb[:], rhs=ag[b][:, :, cols].rearrange("p t n -> p n t"), start=True, stop=True)
+
+        def a_copy(j, q):
+            if q == 0:
+                ai[j] = sbt("ai", [P, HALF * T4], BF16, 4)
+            nc.scalar.copy(out=ai[j][:, q * 1024:(q + 1) * 1024], in_=pa[(j, q)][:])
+
+        def a_quant(j):
+            ca[j] = sbt("ca", [P, HALF], U32, 4)
+            sa[j] = sbt("sa", [P, HALF], U8, 4)
+            quant(ca[j][:], sa[j][:], ai[j][:])
+
+        def m1(j, t):
+            bank = pst("ph", [P, HALF], F32, 4)
+            ph[(j, t)] = bank
+            m = slice(t * P, (t + 1) * P)
+            for k, (c, s) in enumerate(((cx[j], sx[j]), (ca[j], sa[j]))):
+                nc.tensor.matmul_mx(
+                    out=bank[:], lhsT=cw1[:, k, m].bitcast(FP8X4), lhsT_scale=sw1[:, k, m],
+                    rhs=c[:].bitcast(FP8X4), rhs_scale=s[:], start=(k == 0), stop=(k == 1))
+
+        def relu(j, t):
+            if t == 0:
+                hp[j] = sbt("hp", [P, T4, HALF], BF16, 3)
+            nc.scalar.activation(out=hp[j][:, t, :], in_=ph[(j, t)][:], func=ACT.Relu, bias=b1[:, t:t + 1])
+
+        def h_inter(j):
+            hi[j] = sbt("hi", [P, HALF * T4], BF16, 2)
+            interleave(hi[j][:], hp[j][:])
+
+        def h_quant(j):
+            ch[j] = sbt("ch", [P, HALF], U32, 3)
+            sh[j] = sbt("sh", [P, HALF], U8, 3)
+            quant(ch[j][:], sh[j][:], hi[j][:])
+
+        def m2(j, t):
+            bank = pst("pg", [P, HALF], F32, 3)
+            pg[(j, t)] = bank
+            m = slice(t * P, (t + 1) * P)
+            nc.tensor.matmul_mx(
+                out=bank[:], lhsT=cw2[:, m].bitcast(FP8X4), lhsT_scale=sw2[:, m],
+                rhs=ch[j][:].bitcast(FP8X4), rhs_scale=sh[j][:], start=True, stop=True)
+
+        def sig(j, t):
+            if t == 0:
+                gt[j] = sbt("gt", [P, T4, HALF], F32, 3)
+            nc.scalar.activation(out=gt[j][:, t, :], in_=pg[(j, t)][:], func=ACT.Sigmoid, bias=b2[:, t:t + 1])
+
+        def finish(j, t0, t1):
+            b, c0 = j // 2, (j % 2) * HALF
+            g = gt[j][:, t0:t1, :]
+            nc.vector.tensor_tensor(out=g, in0=g, in1=ag[b][:, t0:t1, c0:c0 + HALF], op=ALU.mult)
+            nc.sync.dma_start(
+                out=out[b].rearrange("(p t) h w -> p t (h w)", t=T4)[:, t0:t1, c0:c0 + HALF], in_=g)
+
+        def w_trans(src, k0, tag, nbufs):
+            banks = []
+            for pair in range(2):
+                bank = pst(tag, [P, 2, 2, P], F32, nbufs)
+                banks.append(bank)
+                for a in range(2):
+                    words = src[:, pair * 2 + a, :].bitcast(F32)
+                    for u in range(2):
+                        nc.tensor.transpose(bank[:, a, u, :], words[:, k0 // 2 + u:k0 // 2 + 256:2], idf[:])
+            return banks
+
+        def w_copy(eng, dst, pair, bank):
+            o = dst[:, pair * 1024:(pair + 1) * 1024].bitcast(F32).rearrange("p (a r u) -> p a r u", a=2, u=2)
+            i = bank[:].rearrange("p a u r -> p a r u")
+            if eng == "s":
+                nc.scalar.copy(out=o, in_=i)
+            else:
+                nc.vector.tensor_copy(out=o, in_=i)
+
+        new_xs(0)
+        for h in range(2):
+            c0 = h * HALF
+            widen("s", 0, 0, c0, c0 + HALF)
+            widen("s", 0, 1, c0, c0 + HALF)
+            widen("v", 0, 2, c0, c0 + HALF)
+            widen("v", 0, 3, c0, c0 + HALF)
+            x_inter(h)
+        x_quant(0)
+        x_quant(1)
+        g0 = keep.tile([P, 2048], BF16, name="g0", align_bytes=64)
+        g1 = keep.tile([P, 2048], BF16, name="g1", align_bytes=64)
+        g2 = keep.tile([P, 2048], BF16, name="g2", align_bytes=64)
+        k0 = w_trans(w1, 0, "ph", 4)
+        k1 = w_trans(w1, CH, "ph", 4)
+        w_copy("v", g0[:], 0, k0[0])
+        w_copy("s", g0[:], 1, k0[1])
+        w_copy("v", g1[:], 0, k1[0])
+        w_copy("s", g1[:], 1, k1[1])
+        quant(cw1[:, 0, :], sw1[:, 0, :], g0[:])
+        quant(cw1[:, 1, :], sw1[:, 1, :], g1[:])
+        nc.vector.tensor_copy(out=b1[:], in_=b1h[:])
+        nc.vector.tensor_copy(out=b2[:], in_=b2h[:])
+        for q in range(2):
+            a_fill(0, q, "pg", 3)
+            a_copy(0, q)
+        a_quant(0)
+        k2 = w_trans(w2, 0, "pg", 3)
+        for t in range(T4):
+            m1(0, t)
+        a_fill(1, 0)
+        new_xs(1)
+        for t in range(S_PLANES):
+            widen("v", 1, 2 + t, 0, PIX)
+            widen("s", 1, t, 0, PIX)
+        a_copy(1, 0)
+        a_fill(1, 1)
+        w_copy("v", g2[:], 0, k2[0])
+        w_copy("s", g2[:], 1, k2[1])
+        a_copy(1, 1)
+        a_fill(2, 0)
+        a_quant(1)
+        quant(cw2[:], sw2[:], g2[:])
+
+        load_x(3)
+        load_x(4)
+        for j in range(HALVES + 1):
+            wb, ts = (j + 4) // 2, j % 2
+            if j == 2:
+                load_x(5)
+            if j in (3, 5):
+                load_agg((j + 5) // 2)
+            for t in range(T4):
+                if j < HALVES:
+                    relu(j, t)
+                if j + 1 < HALVES:
+                    m1(j + 1, t)
+            if j == 0:
+                a_copy(2, 0)
+                a_fill(2, 1)
+                a_copy(2, 1)
+                a_fill(3, 0)
+            if j + 3 < HALVES:
+                a_copy(j + 3, 0)
+                a_fill(j + 3, 1)
+            if j + 2 < HALVES:
+                x_inter(j + 2)
+            if wb < IMAGES:
+                if ts == 0:
+                    new_xs(wb)
+                widen("v", wb, S_PLANES + ts, 0, PIX)
+            if j + 2 < HALVES:
+                x_quant(j + 2)
+            if j >= 1:
+                sig(j - 1, 0)
+                m2(j - 1, 3)
+                if j == HALVES:
+                    finish(j - 1, 0, 1)
+                for t in range(1, T4):
+                    sig(j - 1, t)
+                    if j == HALVES:
+                        finish(j - 1, t, t + 1)
+            if wb < IMAGES:
+                widen("s", wb, ts, 0, PIX)
+            if j + 3 < HALVES:
+                a_copy(j + 3, 1)
+            if j < HALVES:
+                h_inter(j)
+            if j + 2 < HALVES:
+                a_quant(j + 2)
+            if j < HALVES:
+                h_quant(j)
+                for t in range(3):
+                    m2(j, t)
+            if j + 4 < HALVES:
+                a_fill(j + 4, 0)
+            if 1 <= j < HALVES:
+                finish(j - 1, 0, T4)

@@ -21,7 +21,7 @@ P = 128
 T4 = 4
 HALF = 512
 HALVES = IMAGES * 2
-S_PLANES = 2
+S_PLANES = (2, 2, 2, 2, 2, 2)
 
 
 def tile_graphaugmentation_pb_t_kernel(tc, x_bytes, x_scale, agg, g1w, g1b, g2w, g2b, out):
@@ -72,14 +72,14 @@ def tile_graphaugmentation_pb_t_kernel(tc, x_bytes, x_scale, agg, g1w, g1b, g2w,
 
         nc.sync.dma_start(out=xsc[:], in_=x_scale.rearrange("o (p t) h w -> p (o t h w)", t=T4))
         load_x(0, 4)
+        load_x(1)
         nc.sync.dma_start(out=w1[:], in_=g1w.rearrange("(m t) k -> m t k", t=T4))
         load_agg(0, 2)
         nc.sync.dma_start(out=b1h[:], in_=g1b.rearrange("(p t) -> p t", t=T4))
         nc.sync.dma_start(out=b2h[:], in_=g2b.rearrange("(p t) -> p t", t=T4))
-        load_x(1)
         nc.sync.dma_start(out=w2[:], in_=g2w.rearrange("(m t) k -> m t k", t=T4))
-        load_agg(1)
         load_x(2)
+        load_agg(1)
         load_agg(2)
         load_agg(3)
 
@@ -113,24 +113,29 @@ def tile_graphaugmentation_pb_t_kernel(tc, x_bytes, x_scale, agg, g1w, g1b, g2w,
             nc.vector.quantize_mx(out=codes.bitcast(FP8X4), scales=scales, in_=src)
 
         def x_quant(j):
-            cx[j] = sbt("cx", [P, HALF], U32, 4)
-            sx[j] = sbt("sx", [P, HALF], U8, 4)
+            cx[j] = sbt("cx", [P, HALF], U32, 5)
+            sx[j] = sbt("sx", [P, HALF], U8, 5)
             quant(cx[j][:], sx[j][:], xi[j][:])
 
-        def a_fill(j, q, tag="pa", bufs=1):
+        def a_fill(j, q, tag="pa", bufs=2):
             b, c0 = j // 2, (j % 2) * HALF + q * 256
             bank = pst(tag, [P, 1024], BF16, bufs)
             pa[(j, q)] = bank
             for r in range(2):
                 cols = slice(c0 + r * P, c0 + r * P + P)
                 nc.tensor.matmul(
-                    out=bank[:, r * 512:(r + 1) * 512].rearrange("p (n t) -> p n t", t=T4),
-                    lhsT=idb[:], rhs=ag[b][:, :, cols].rearrange("p t n -> p n t"), start=True, stop=True)
+                    out=bank[:, r * 512:(r + 1) * 512].rearrange("p (c i t) -> p c t i", i=8, t=T4),
+                    lhsT=idb[:], rhs=ag[b][:, :, cols].rearrange("p t (c i) -> p c t i", i=8), start=True, stop=True)
 
         def a_copy(j, q):
             if q == 0:
                 ai[j] = sbt("ai", [P, HALF * T4], BF16, 4)
             nc.scalar.copy(out=ai[j][:, q * 1024:(q + 1) * 1024], in_=pa[(j, q)][:])
+
+        def a_inter(j):
+            b, c0 = j // 2, (j % 2) * HALF
+            ai[j] = sbt("ai", [P, HALF * T4], BF16, 4)
+            interleave(ai[j][:], ag[b][:, :, c0:c0 + HALF])
 
         def a_quant(j):
             ca[j] = sbt("ca", [P, HALF], U32, 4)
@@ -138,7 +143,7 @@ def tile_graphaugmentation_pb_t_kernel(tc, x_bytes, x_scale, agg, g1w, g1b, g2w,
             quant(ca[j][:], sa[j][:], ai[j][:])
 
         def m1(j, t):
-            bank = pst("ph", [P, HALF], F32, 4)
+            bank = pst("ph", [P, HALF], F32, 3)
             ph[(j, t)] = bank
             m = slice(t * P, (t + 1) * P)
             for k, (c, s) in enumerate(((cx[j], sx[j]), (ca[j], sa[j]))):
@@ -202,98 +207,107 @@ def tile_graphaugmentation_pb_t_kernel(tc, x_bytes, x_scale, agg, g1w, g1b, g2w,
         new_xs(0)
         for h in range(2):
             c0 = h * HALF
-            widen("s", 0, 0, c0, c0 + HALF)
-            widen("s", 0, 1, c0, c0 + HALF)
-            widen("v", 0, 2, c0, c0 + HALF)
-            widen("v", 0, 3, c0, c0 + HALF)
-            x_inter(h)
+            for t in range(T4):
+                widen("s" if t in (1, 3) else "v", 0, t, c0, c0 + HALF)
+        x_inter(0)
+        new_xs(1)
+        widen("s", 1, 0, 0, PIX)
+        widen("v", 1, 3, 0, PIX)
+        x_inter(1)
         x_quant(0)
+        widen("s", 1, 1, 0, PIX)
         x_quant(1)
         g0 = keep.tile([P, 2048], BF16, name="g0", align_bytes=64)
         g1 = keep.tile([P, 2048], BF16, name="g1", align_bytes=64)
         g2 = keep.tile([P, 2048], BF16, name="g2", align_bytes=64)
-        k0 = w_trans(w1, 0, "ph", 4)
-        k1 = w_trans(w1, CH, "ph", 4)
+        k0 = w_trans(w1, 0, "ph", 3)
+        k1 = w_trans(w1, CH, "pg", 3)
         w_copy("v", g0[:], 0, k0[0])
         w_copy("s", g0[:], 1, k0[1])
-        w_copy("v", g1[:], 0, k1[0])
+        w_copy("s", g1[:], 0, k1[0])
+        widen("v", 1, 2, 0, PIX)
         w_copy("s", g1[:], 1, k1[1])
         quant(cw1[:, 0, :], sw1[:, 0, :], g0[:])
+        a_inter(0)
         quant(cw1[:, 1, :], sw1[:, 1, :], g1[:])
+        a_quant(0)
+        a_fill(1, 0)
+        a_fill(1, 1)
+        k2 = w_trans(w2, 0, "pg", 3)
+        for t in range(3):
+            m1(0, t)
+        a_copy(1, 0)
+        a_copy(1, 1)
+        x_inter(2)
         nc.vector.tensor_copy(out=b1[:], in_=b1h[:])
         nc.vector.tensor_copy(out=b2[:], in_=b2h[:])
-        for q in range(2):
-            a_fill(0, q, "pg", 3)
-            a_copy(0, q)
-        a_quant(0)
-        k2 = w_trans(w2, 0, "pg", 3)
-        for t in range(T4):
-            m1(0, t)
-        a_fill(1, 0)
-        new_xs(1)
-        for t in range(S_PLANES):
-            widen("v", 1, 2 + t, 0, PIX)
-            widen("s", 1, t, 0, PIX)
-        a_copy(1, 0)
-        a_fill(1, 1)
-        w_copy("v", g2[:], 0, k2[0])
+        w_copy("s", g2[:], 0, k2[0])
         w_copy("s", g2[:], 1, k2[1])
-        a_copy(1, 1)
-        a_fill(2, 0)
         a_quant(1)
+        x_quant(2)
+        x_inter(3)
         quant(cw2[:], sw2[:], g2[:])
+        new_xs(2)
+        widen("v", 2, 3, 0, PIX)
+        widen("s", 2, 0, 0, PIX)
+        x_quant(3)
+        a_inter(2)
+        a_fill(3, 0)
+        a_fill(3, 1)
 
         load_x(3)
         load_x(4)
         for j in range(HALVES + 1):
-            wb, ts = (j + 4) // 2, j % 2
-            if j == 2:
+            wb, ts = (j + 5) // 2, (j + 1) % 2
+            last = j == HALVES
+            if j == 1:
                 load_x(5)
             if j in (3, 5):
                 load_agg((j + 5) // 2)
             for t in range(T4):
-                if j < HALVES:
+                if not last:
                     relu(j, t)
-                if j + 1 < HALVES:
-                    m1(j + 1, t)
-            if j == 0:
-                a_copy(2, 0)
-                a_fill(2, 1)
-                a_copy(2, 1)
-                a_fill(3, 0)
-            if j + 3 < HALVES:
-                a_copy(j + 3, 0)
-                a_fill(j + 3, 1)
-            if j + 2 < HALVES:
-                x_inter(j + 2)
+                if t == 0:
+                    if not last:
+                        m1(j, 3)
+                elif j + 1 < HALVES:
+                    m1(j + 1, t - 1)
+            if 1 <= j < HALVES - 3:
+                x_inter(j + 3)
+            planes = []
             if wb < IMAGES:
+                planes = [(0, 3), (1, 2)][ts]
                 if ts == 0:
                     new_xs(wb)
-                widen("v", wb, S_PLANES + ts, 0, PIX)
-            if j + 2 < HALVES:
-                x_quant(j + 2)
-            if j >= 1:
-                sig(j - 1, 0)
-                m2(j - 1, 3)
-                if j == HALVES:
-                    finish(j - 1, 0, 1)
-                for t in range(1, T4):
-                    sig(j - 1, t)
-                    if j == HALVES:
-                        finish(j - 1, t, t + 1)
-            if wb < IMAGES:
-                widen("s", wb, ts, 0, PIX)
-            if j + 3 < HALVES:
-                a_copy(j + 3, 1)
-            if j < HALVES:
-                h_inter(j)
+            for t in planes:
+                if t >= S_PLANES[wb]:
+                    widen("v", wb, t, 0, PIX)
             if j + 2 < HALVES:
                 a_quant(j + 2)
-            if j < HALVES:
+            if j >= 1:
+                for t in range(T4):
+                    sig(j - 1, t)
+                    if t == 0:
+                        m2(j - 1, 3)
+                        if j + 3 < HALVES:
+                            a_fill(j + 3, 0)
+                            a_fill(j + 3, 1)
+                    if last:
+                        finish(j - 1, t, t + 1)
+            if not last:
+                h_inter(j)
+            if j + 3 < HALVES:
+                a_copy(j + 3, 0)
+            for t in planes:
+                if t < S_PLANES[wb]:
+                    widen("s", wb, t, 0, PIX)
+            if j + 3 < HALVES:
+                a_copy(j + 3, 1)
+            if 1 <= j < HALVES - 3:
+                x_quant(j + 3)
+            if not last:
                 h_quant(j)
                 for t in range(3):
                     m2(j, t)
-            if j + 4 < HALVES:
-                a_fill(j + 4, 0)
             if 1 <= j < HALVES:
                 finish(j - 1, 0, T4)

@@ -21,7 +21,7 @@ P = 128
 T4 = 4
 HALF = 512
 HALVES = IMAGES * 2
-S_PLANES = (2, 2, 2, 2, 2, 2)
+S_PLANES = (2, 2, 3, 3, 3, 3)
 
 
 def tile_graphaugmentation_pb_t_kernel(tc, x_bytes, x_scale, agg, g1w, g1b, g2w, g2b, out):
@@ -248,7 +248,7 @@ def tile_graphaugmentation_pb_t_kernel(tc, x_bytes, x_scale, agg, g1w, g1b, g2w,
         x_inter(3)
         quant(cw2[:], sw2[:], g2[:])
         new_xs(2)
-        widen("v", 2, 3, 0, PIX)
+        widen("s", 2, 1, 0, PIX)
         widen("s", 2, 0, 0, PIX)
         x_quant(3)
         a_inter(2)
@@ -260,6 +260,8 @@ def tile_graphaugmentation_pb_t_kernel(tc, x_bytes, x_scale, agg, g1w, g1b, g2w,
         for j in range(HALVES + 1):
             wb, ts = (j + 5) // 2, (j + 1) % 2
             last = j == HALVES
+            nx, nq, na = j + 3, j + 2, j + 3
+            tens = na < HALVES and na % 2 == 1
             if j == 1:
                 load_x(5)
             if j in (3, 5):
@@ -272,42 +274,43 @@ def tile_graphaugmentation_pb_t_kernel(tc, x_bytes, x_scale, agg, g1w, g1b, g2w,
                         m1(j, 3)
                 elif j + 1 < HALVES:
                     m1(j + 1, t - 1)
-            if 1 <= j < HALVES - 3:
-                x_inter(j + 3)
+            if 4 <= nx < HALVES:
+                x_inter(nx)
             planes = []
             if wb < IMAGES:
-                planes = [(0, 3), (1, 2)][ts]
+                planes = [(0, 1), (2, 3)][ts]
                 if ts == 0:
                     new_xs(wb)
             for t in planes:
                 if t >= S_PLANES[wb]:
                     widen("v", wb, t, 0, PIX)
-            if j + 2 < HALVES:
-                a_quant(j + 2)
+            if nq < HALVES:
+                a_quant(nq)
             if j >= 1:
                 for t in range(T4):
                     sig(j - 1, t)
                     if t == 0:
                         m2(j - 1, 3)
-                        if j + 3 < HALVES:
-                            a_fill(j + 3, 0)
-                            a_fill(j + 3, 1)
+                        if tens:
+                            a_fill(na, 0)
+                            a_fill(na, 1)
                     if last:
                         finish(j - 1, t, t + 1)
             if not last:
                 h_inter(j)
-            if j + 3 < HALVES:
-                a_copy(j + 3, 0)
             for t in planes:
                 if t < S_PLANES[wb]:
                     widen("s", wb, t, 0, PIX)
-            if j + 3 < HALVES:
-                a_copy(j + 3, 1)
-            if 1 <= j < HALVES - 3:
-                x_quant(j + 3)
+            if tens:
+                a_copy(na, 0)
+                a_copy(na, 1)
+            if 4 <= nx < HALVES:
+                x_quant(nx)
             if not last:
                 h_quant(j)
                 for t in range(3):
                     m2(j, t)
+            if na < HALVES and na % 2 == 0:
+                a_inter(na)
             if 1 <= j < HALVES:
                 finish(j - 1, 0, T4)

from contextlib import ExitStack

import concourse.mybir as mybir
from concourse.masks import make_identity

IMAGES, CH, ROWS, COLS = 6, 512, 32, 32
PIX = ROWS * COLS
HID = 512
FLOPS = 2 * IMAGES * PIX * (HID * 2 * CH + CH * HID)

F32 = mybir.dt.float32
BF16 = mybir.dt.bfloat16
U32 = mybir.dt.uint32
U8 = mybir.dt.uint8
FP8 = mybir.dt.float8_e4m3fn
FP8X4 = mybir.dt.float8_e4m3fn_x4
ACT = mybir.ActivationFunctionType
ALU = mybir.AluOpType

P = 128
T4 = 4
HALF = 512
HALVES = IMAGES * 2
S_PLANES = (2, 2, 3, 3, 3, 3)


def tile_graphaugmentation_pb_t_kernel(tc, x_bytes, x_scale, agg, g1w, g1b, g2w, g2b, out):
    nc = tc.nc
    with ExitStack() as ctx:
        keep = ctx.enter_context(tc.tile_pool(name="keep", bufs=1))
        sb = ctx.enter_context(tc.tile_pool(name="sb", bufs=2))
        ps = ctx.enter_context(tc.psum_pool(name="ps", bufs=1))
        ctx.enter_context(tc.manual_schedule())

        def sbt(tag, shape, dtype, bufs):
            return sb.tile(shape, dtype, name=tag, tag=tag, bufs=bufs, align_bytes=64)

        def pst(tag, shape, dtype, bufs):
            return ps.tile(shape, dtype, name=tag, tag=tag, bufs=bufs)

        xb, ag, xs, xi, ai, cx, sx, ca, sa = {}, {}, {}, {}, {}, {}, {}, {}, {}
        hp, hi, ch, sh, gt, ph, pg, pa = {}, {}, {}, {}, {}, {}, {}, {}

        def load_x(b, pieces=1):
            xb[b] = sbt("xb", [P, T4, PIX], U8, 3)
            src = x_bytes[b].rearrange("(p t) h w -> p t (h w)", t=T4)
            n = T4 // pieces
            for i in range(pieces):
                nc.sync.dma_start(out=xb[b][:, i * n:(i + 1) * n, :], in_=src[:, i * n:(i + 1) * n, :])

        def load_agg(b, pieces=1):
            ag[b] = sbt("ag", [P, T4, PIX], BF16, 4)
            src = agg[b].rearrange("(p t) h w -> p t (h w)", t=T4)
            n = PIX // pieces
            for i in range(pieces):
                nc.sync.dma_start(out=ag[b][:, :, i * n:(i + 1) * n], in_=src[:, :, i * n:(i + 1) * n])

        xsc = keep.tile([P, T4], F32, name="xsc")
        b1h = keep.tile([P, T4], BF16, name="b1h")
        b2h = keep.tile([P, T4], BF16, name="b2h")
        b1 = keep.tile([P, T4], F32, name="b1")
        b2 = keep.tile([P, T4], F32, name="b2")
        w1 = keep.tile([P, T4, 2 * CH], BF16, name="w1", align_bytes=64)
        w2 = keep.tile([P, T4, HID], BF16, name="w2", align_bytes=64)
        cw1 = keep.tile([P, 2, HID], U32, name="cw1", align_bytes=64)
        sw1 = keep.tile([P, 2, HID], U8, name="sw1", align_bytes=64)
        cw2 = keep.tile([P, CH], U32, name="cw2", align_bytes=64)
        sw2 = keep.tile([P, CH], U8, name="sw2", align_bytes=64)
        idf = keep.tile([P, P], F32, name="idf", align_bytes=64)
        idb = keep.tile([P, P], BF16, name="idb", align_bytes=64)
        warm = keep.tile([P, 1], F32, name="warm")

        nc.sync.dma_start(out=xsc[:], in_=x_scale.rearrange("o (p t) h w -> p (o t h w)", t=T4))
        load_x(0, 4)
        load_x(1)
        nc.sync.dma_start(out=w1[:], in_=g1w.rearrange("(m t) k -> m t k", t=T4))
        load_agg(0, 2)
        nc.sync.dma_start(out=b1h[:], in_=g1b.rearrange("(p t) -> p t", t=T4))
        nc.sync.dma_start(out=b2h[:], in_=g2b.rearrange("(p t) -> p t", t=T4))
        nc.sync.dma_start(out=w2[:], in_=g2w.rearrange("(m t) k -> m t k", t=T4))
        load_x(2)
        load_agg(1)
        load_agg(2)
        load_agg(3)

        nc.gpsimd.memset(warm[:], 0.0)
        nc.scalar.activation(out=warm[:], in_=warm[:], func=ACT.Sigmoid)
        make_identity(nc, idf[:])
        make_identity(nc, idb[:])

        def new_xs(b):
            xs[b] = sbt("xs", [P, T4, PIX], BF16, 2)

        def widen(eng, b, t, c0, c1):
            src = xb[b][:, t, c0:c1].bitcast(FP8)
            dst = xs[b][:, t, c0:c1]
            if eng == "s":
                nc.scalar.activation(out=dst, in_=src, func=ACT.Copy, scale=xsc[:, t:t + 1])
            else:
                nc.vector.tensor_scalar(out=dst, in0=src, scalar1=xsc[:, t:t + 1], scalar2=None, op0=ALU.mult)

        def interleave(dst, src):
            nc.vector.tensor_copy(
                out=dst.rearrange("p (c i t) -> p c t i", i=4, t=T4),
                in_=src.rearrange("p t (c i) -> p c t i", i=4))

        def x_inter(j):
            b, c0 = j // 2, (j % 2) * HALF
            xi[j] = sbt("xi", [P, HALF * T4], BF16, 3)
            interleave(xi[j][:], xs[b][:, :, c0:c0 + HALF])

        def quant(codes, scales, src):
            nc.vector.quantize_mx(out=codes.bitcast(FP8X4), scales=scales, in_=src)

        def x_quant(j):
            cx[j] = sbt("cx", [P, HALF], U32, 5)
            sx[j] = sbt("sx", [P, HALF], U8, 5)
            quant(cx[j][:], sx[j][:], xi[j][:])

        def a_fill(j, q, tag="pa", bufs=2):
            b, c0 = j // 2, (j % 2) * HALF + q * 256
            bank = pst(tag, [P, 1024], BF16, bufs)
            pa[(j, q)] = bank
            for r in range(2):
                cols = slice(c0 + r * P, c0 + r * P + P)
                nc.tensor.matmul(
                    out=bank[:, r * 512:(r + 1) * 512].rearrange("p (c i t) -> p c t i", i=8, t=T4),
                    lhsT=idb[:], rhs=ag[b][:, :, cols].rearrange("p t (c i) -> p c t i", i=8), start=True, stop=True)

        def a_copy(j, q):
            if q == 0:
                ai[j] = sbt("ai", [P, HALF * T4], BF16, 4)
            nc.scalar.copy(out=ai[j][:, q * 1024:(q + 1) * 1024], in_=pa[(j, q)][:])

        def a_inter(j):
            b, c0 = j // 2, (j % 2) * HALF
            ai[j] = sbt("ai", [P, HALF * T4], BF16, 4)
            interleave(ai[j][:], ag[b][:, :, c0:c0 + HALF])

        def a_quant(j):
            ca[j] = sbt("ca", [P, HALF], U32, 4)
            sa[j] = sbt("sa", [P, HALF], U8, 4)
            quant(ca[j][:], sa[j][:], ai[j][:])

        def m1(j, t):
            bank = pst("ph", [P, HALF], F32, 3)
            ph[(j, t)] = bank
            m = slice(t * P, (t + 1) * P)
            for k, (c, s) in enumerate(((cx[j], sx[j]), (ca[j], sa[j]))):
                nc.tensor.matmul_mx(
                    out=bank[:], lhsT=cw1[:, k, m].bitcast(FP8X4), lhsT_scale=sw1[:, k, m],
                    rhs=c[:].bitcast(FP8X4), rhs_scale=s[:], start=(k == 0), stop=(k == 1))

        def relu(j, t):
            if t == 0:
                hp[j] = sbt("hp", [P, T4, HALF], BF16, 3)
            nc.scalar.activation(out=hp[j][:, t, :], in_=ph[(j, t)][:], func=ACT.Relu, bias=b1[:, t:t + 1])

        def h_inter(j):
            hi[j] = sbt("hi", [P, HALF * T4], BF16, 2)
            interleave(hi[j][:], hp[j][:])

        def h_quant(j):
            ch[j] = sbt("ch", [P, HALF], U32, 3)
            sh[j] = sbt("sh", [P, HALF], U8, 3)
            quant(ch[j][:], sh[j][:], hi[j][:])

        def m2(j, t):
            bank = pst("pg", [P, HALF], F32, 3)
            pg[(j, t)] = bank
            m = slice(t * P, (t + 1) * P)
            nc.tensor.matmul_mx(
                out=bank[:], lhsT=cw2[:, m].bitcast(FP8X4), lhsT_scale=sw2[:, m],
                rhs=ch[j][:].bitcast(FP8X4), rhs_scale=sh[j][:], start=True, stop=True)

        def sig(j, t):
            if t == 0:
                gt[j] = sbt("gt", [P, T4, HALF], F32, 3)
            nc.scalar.activation(out=gt[j][:, t, :], in_=pg[(j, t)][:], func=ACT.Sigmoid, bias=b2[:, t:t + 1])

        def finish(j, t0, t1):
            b, c0 = j // 2, (j % 2) * HALF
            g = gt[j][:, t0:t1, :]
            nc.vector.tensor_tensor(out=g, in0=g, in1=ag[b][:, t0:t1, c0:c0 + HALF], op=ALU.mult)
            nc.sync.dma_start(
                out=out[b].rearrange("(p t) h w -> p t (h w)", t=T4)[:, t0:t1, c0:c0 + HALF], in_=g)

        def w_trans(src, k0, tag, nbufs):
            banks = []
            for pair in range(2):
                bank = pst(tag, [P, 2, 2, P], F32, nbufs)
                banks.append(bank)
                for a in range(2):
                    words = src[:, pair * 2 + a, :].bitcast(F32)
                    for u in range(2):
                        nc.tensor.transpose(bank[:, a, u, :], words[:, k0 // 2 + u:k0 // 2 + 256:2], idf[:])
            return banks

        def w_copy(eng, dst, pair, bank):
            o = dst[:, pair * 1024:(pair + 1) * 1024].bitcast(F32).rearrange("p (a r u) -> p a r u", a=2, u=2)
            i = bank[:].rearrange("p a u r -> p a r u")
            if eng == "s":
                nc.scalar.copy(out=o, in_=i)
            else:
                nc.vector.tensor_copy(out=o, in_=i)

        new_xs(0)
        for h in range(2):
            c0 = h * HALF
            for t in range(T4):
                widen("s" if t in (1, 3) else "v", 0, t, c0, c0 + HALF)
        x_inter(0)
        new_xs(1)
        widen("s", 1, 0, 0, PIX)
        widen("v", 1, 3, 0, PIX)
        x_inter(1)
        x_quant(0)
        widen("s", 1, 1, 0, PIX)
        x_quant(1)
        g0 = keep.tile([P, 2048], BF16, name="g0", align_bytes=64)
        g1 = keep.tile([P, 2048], BF16, name="g1", align_bytes=64)
        g2 = keep.tile([P, 2048], BF16, name="g2", align_bytes=64)
        k0 = w_trans(w1, 0, "ph", 3)
        k1 = w_trans(w1, CH, "pg", 3)
        w_copy("v", g0[:], 0, k0[0])
        w_copy("s", g0[:], 1, k0[1])
        w_copy("s", g1[:], 0, k1[0])
        widen("v", 1, 2, 0, PIX)
        w_copy("s", g1[:], 1, k1[1])
        quant(cw1[:, 0, :], sw1[:, 0, :], g0[:])
        a_inter(0)
        quant(cw1[:, 1, :], sw1[:, 1, :], g1[:])
        a_quant(0)
        a_fill(1, 0)
        a_fill(1, 1)
        k2 = w_trans(w2, 0, "pg", 3)
        for t in range(3):
            m1(0, t)
        a_copy(1, 0)
        a_copy(1, 1)
        x_inter(2)
        nc.vector.tensor_copy(out=b1[:], in_=b1h[:])
        nc.vector.tensor_copy(out=b2[:], in_=b2h[:])
        w_copy("s", g2[:], 0, k2[0])
        w_copy("s", g2[:], 1, k2[1])
        a_quant(1)
        x_quant(2)
        x_inter(3)
        quant(cw2[:], sw2[:], g2[:])
        new_xs(2)
        widen("s", 2, 1, 0, PIX)
        widen("s", 2, 0, 0, PIX)
        x_quant(3)
        a_inter(2)
        a_fill(3, 0)
        a_fill(3, 1)

        load_x(3)
        load_x(4)
        for j in range(HALVES + 1):
            wb, ts = (j + 5) // 2, (j + 1) % 2
            last = j == HALVES
            nx, nq, na = j + 3, j + 2, j + 3
            tens = na < HALVES and na % 2 == 1
            if j == 1:
                load_x(5)
            if j in (3, 5):
                load_agg((j + 5) // 2)
            for t in range(T4):
                if not last:
                    relu(j, t)
                if t == 0:
                    if not last:
                        m1(j, 3)
                elif j + 1 < HALVES:
                    m1(j + 1, t - 1)
            if 4 <= nx < HALVES:
                x_inter(nx)
            planes = []
            if wb < IMAGES:
                planes = [(0, 1), (2, 3)][ts]
                if ts == 0:
                    new_xs(wb)
            for t in planes:
                if t >= S_PLANES[wb]:
                    widen("v", wb, t, 0, PIX)
            if nq < HALVES:
                a_quant(nq)
            if j >= 1:
                for t in range(T4):
                    sig(j - 1, t)
                    if t == 0:
                        m2(j - 1, 3)
                        if tens:
                            a_fill(na, 0)
                            a_fill(na, 1)
                    if last:
                        finish(j - 1, t, t + 1)
            if not last:
                h_inter(j)
            for t in planes:
                if t < S_PLANES[wb]:
                    widen("s", wb, t, 0, PIX)
            if tens:
                a_copy(na, 0)
                a_copy(na, 1)
            if 4 <= nx < HALVES:
                x_quant(nx)
            if not last:
                h_quant(j)
                for t in range(3):
                    m2(j, t)
            if na < HALVES and na % 2 == 0:
                a_inter(na)
            if 1 <= j < HALVES:
                finish(j - 1, 0, T4)
